import numpy as np
import ml_dtypes


def mxq(x, axis, fmt="e4m3"):
    dtype, down = {"e4m3": (ml_dtypes.float8_e4m3fn, 7), "e5m2": (ml_dtypes.float8_e5m2, 14)}[fmt]
    v = np.moveaxis(np.asarray(x, np.float32).astype(ml_dtypes.bfloat16).astype(np.float64), axis, -1)
    blocks = v.reshape(v.shape[:-1] + (-1, 32))
    amax = np.abs(blocks).max(-1, keepdims=True)
    byte = np.maximum(np.where(amax > 0, np.frexp(amax)[1] - 1 + 127, 0) - down, 1)
    scale = np.exp2(byte - 127.0)
    codes = (blocks / scale).astype(np.float32).astype(dtype).astype(np.float64)
    return np.moveaxis((codes * scale).reshape(v.shape), -1, axis)


WIDE = False


def mx_kscale(k):
    if not WIDE:
        return np.ones(k)
    levels = np.array([10, -10, 5, -5, 0])
    a = np.random.permutation(np.resize(levels, k // 512 * 4)).reshape(k // 512, 4)
    idx = np.arange(k)
    return np.exp2(a[idx // 512, idx % 128 // 32])


BF16 = ml_dtypes.bfloat16


def bf(x):
    return np.asarray(x, np.float32).astype(BF16)


def f64(x):
    return np.asarray(x).astype(np.float64)


B, S, D_IN, MID, FFN, D_OUT, R = 8, 1024, 256, 512, 512, 256, 16
LN_EPS = 1e-5


def silu(v):
    return v / (1.0 + np.exp(-v))


def layer_norm(x, gamma, beta):
    m = np.mean(x, axis=-1, keepdims=True)
    v = np.mean(np.square(x - m), axis=-1, keepdims=True)
    return (x - m) / np.sqrt(v + LN_EPS) * gamma + beta


def setup_inputs():
    t, s = mx_kscale(FFN), mx_kscale(MID)
    return {"h": bf(silu(np.random.standard_normal((B, S, FFN))) * t),
            "w_f2": bf(np.random.standard_normal((MID, FFN)) / np.sqrt(FFN) / t),
            "b_f2": bf(0.1 * np.random.standard_normal(MID)),
            "res1": bf(0.7 * np.random.standard_normal((B, S, MID))),
            "g2": bf((1.0 + 0.1 * np.random.standard_normal(MID)) * s),
            "be2": bf(0.1 * np.random.standard_normal(MID) * s),
            "w_h": bf(np.random.standard_normal((D_OUT, MID)) / np.sqrt(MID) / s),
            "b_h": bf(0.1 * np.random.standard_normal(D_OUT))}


def reference(h, w_f2, b_f2, res1, g2, be2, w_h, b_h):
    ffn = (mxq(f64(h), 2, "e4m3") @ mxq(f64(w_f2), 1, "e4m3").T) + f64(b_f2)
    res2 = f64(res1) + ffn
    norm2 = layer_norm(res2, f64(g2), f64(be2))
    return (mxq(norm2, 2, "e4m3") @ mxq(f64(w_h), 1, "e4m3").T) + f64(b_h)

@@ -1,0 +1,267 @@
+from contextlib import ExitStack
+
+import concourse.mybir as mybir
+from concourse.masks import make_identity
+
+F32 = mybir.dt.float32
+BF16 = mybir.dt.bfloat16
+U32 = mybir.dt.uint32
+U8 = mybir.dt.uint8
+FP8X4 = mybir.dt.float8_e4m3fn_x4
+ADD = mybir.AluOpType.add
+MULT = mybir.AluOpType.mult
+ACT = mybir.ActivationFunctionType
+
+P = 128
+PACK = 4
+TOKENS = 8 * 1024
+FFN = 512
+MID = 512
+D_OUT = 256
+LN_EPS = 1e-5
+GROUP = 4
+GROUPS = TOKENS // (P * GROUP)
+
+FLOPS = 2 * TOKENS * FFN * MID + 2 * TOKENS * MID * D_OUT
+
+
+def transpose_bf16_rows(nc, psum, work, rows, ident):
+    words = rows.bitcast(F32)
+    pair_grouped = work.tile([P, GROUP * P * PACK], BF16, align_bytes=64)
+    grouped_words = pair_grouped[:].bitcast(F32).rearrange("p (j r u) -> p j r u", j=GROUP, u=2)
+    for b in range(GROUP // 2):
+        pairs_t = psum.tile([P, 4 * P], F32)
+        for j in range(2):
+            for u in range(2):
+                first = ((2 * b + j) * 2 + u) * P
+                nc.tensor.transpose(pairs_t[:, (2 * j + u) * P : (2 * j + u + 1) * P], words[:, first : first + P], ident)
+        nc.scalar.copy(
+            out=grouped_words[:, 2 * b : 2 * b + 2],
+            in_=pairs_t[:].rearrange("p (j u r) -> p j r u", j=2, u=2),
+        )
+    return pair_grouped
+
+
+def transpose_f32_rows(nc, psum, work, row_tiles, ident, gain, shift):
+    width = len(row_tiles) * P
+    planes = work.tile([P, PACK, width], BF16)
+    for c in range(PACK):
+        chunk_t = psum.tile([P, width], F32)
+        for r, x in enumerate(row_tiles):
+            nc.tensor.transpose(chunk_t[:, r * P : (r + 1) * P], x[:, c * P : (c + 1) * P], ident)
+        nc.scalar.activation(out=planes[:, c, :], in_=chunk_t[:], func=ACT.Identity, scale=gain[c], bias=shift[c])
+    chunk_grouped = work.tile([P, width * PACK], BF16, align_bytes=64)
+    nc.scalar.copy(
+        out=chunk_grouped[:].rearrange("p (w i c) -> p w c i", i=4, c=PACK),
+        in_=planes[:].rearrange("p c (w i) -> p w c i", i=4),
+    )
+    return chunk_grouped
+
+
+def tile_tsh_mid_block_pb_t_kernel(tc, h, w_f2, b_f2, res1, g2, be2, w_h, b_h, out):
+    nc = tc.nc
+    h_rows = h.flatten_outer_dims().rearrange("(p j) k -> p (j k)", p=P)
+    res_rows = res1.flatten_outer_dims().rearrange("(p j) m -> p (j m)", p=P)
+    out_rows = out.flatten_outer_dims().rearrange("(p j) o -> p (j o)", p=P)
+
+    with ExitStack() as ctx:
+        const = ctx.enter_context(tc.tile_pool(name="const", bufs=1))
+        loads = ctx.enter_context(tc.tile_pool(name="loads", bufs=4))
+        work = ctx.enter_context(tc.tile_pool(name="work", bufs=3))
+        psum = ctx.enter_context(tc.psum_pool(name="psum", bufs=2))
+
+        ident = const.tile([P, P], F32)
+        make_identity(nc, ident[:])
+        eps = const.tile([P, 1], F32)
+        nc.vector.memset(eps[:], LN_EPS)
+
+        w1_sb = const.tile([P, GROUP * FFN], BF16)
+        nc.sync.dma_start(
+            out=w1_sb[:].rearrange("p (r k) -> p r k", r=GROUP), in_=w_f2.rearrange("(r p) k -> p r k", p=P)
+        )
+        w1_codes = const.tile([P, MID], U32, align_bytes=64)
+        w1_scales = const.tile([P, MID], U8, align_bytes=64)
+        w1_grouped = transpose_bf16_rows(nc, psum, work, w1_sb[:], ident[:])
+        nc.vector.quantize_mx(out=w1_codes[:].bitcast(FP8X4), scales=w1_scales[:], in_=w1_grouped[:])
+
+        bias_rows = const.tile([P, MID + D_OUT], BF16)
+        nc.vector.memset(bias_rows[:], 0.0)
+        nc.scalar.dma_start(out=bias_rows[0:1, 0:MID], in_=b_f2.rearrange("(o m) -> o m", o=1))
+        nc.scalar.dma_start(out=bias_rows[0:1, MID : MID + D_OUT], in_=b_h.rearrange("(o m) -> o m", o=1))
+        ones = const.tile([P, P], BF16)
+        nc.vector.memset(ones[:], 1.0)
+        b1_all = const.tile([P, MID], F32)
+        b1_spread = psum.tile([P, MID], F32, tag="ffn")
+        nc.tensor.matmul(out=b1_spread[:], lhsT=ones[:], rhs=bias_rows[:, 0:MID], start=True, stop=True)
+        nc.vector.tensor_copy(out=b1_all[:], in_=b1_spread[:])
+        b2_all = const.tile([P, D_OUT], F32)
+        b2_spread = psum.tile([P, D_OUT], F32, tag="ffn")
+        nc.tensor.matmul(out=b2_spread[:], lhsT=ones[:], rhs=bias_rows[:, MID : MID + D_OUT], start=True, stop=True)
+        nc.vector.tensor_copy(out=b2_all[:], in_=b2_spread[:])
+
+        vec_rows = const.tile([P, P], BF16)
+        nc.vector.memset(vec_rows[:], 0.0)
+        nc.scalar.dma_start(out=vec_rows[0:PACK, :], in_=g2.rearrange("(c p) -> c p", p=P))
+        nc.scalar.dma_start(out=vec_rows[PACK : 2 * PACK, :], in_=be2.rearrange("(c p) -> c p", p=P))
+        vec_rows_f32 = const.tile([P, P], F32)
+        nc.vector.tensor_copy(out=vec_rows_f32[:], in_=vec_rows[:])
+        vec_t = psum.tile([P, P], F32, tag="chunk_t")
+        nc.tensor.transpose(vec_t[:], vec_rows_f32[:], ident[:])
+        vec_cols = const.tile([P, 2 * PACK], F32)
+        nc.vector.tensor_copy(out=vec_cols[:], in_=vec_t[:, 0 : 2 * PACK])
+        gain = [vec_cols[:, c : c + 1] for c in range(PACK)]
+        shift = [vec_cols[:, PACK + c : PACK + c + 1] for c in range(PACK)]
+
+        w2_sb = const.tile([P, D_OUT // P, MID], BF16)
+        nc.scalar.dma_start(out=w2_sb[:], in_=w_h.rearrange("(r p) m -> p r m", p=P))
+        w2_f32 = const.tile([P, D_OUT // P, MID], F32)
+        nc.vector.tensor_copy(out=w2_f32[:], in_=w2_sb[:])
+        w2_codes = const.tile([P, D_OUT], U32, align_bytes=64)
+        w2_scales = const.tile([P, D_OUT], U8, align_bytes=64)
+        w2_grouped = transpose_f32_rows(
+            nc, psum, work, [w2_f32[:, r, :] for r in range(D_OUT // P)], ident[:], [1.0] * PACK, [0.0] * PACK
+        )
+        nc.vector.quantize_mx(out=w2_codes[:].bitcast(FP8X4), scales=w2_scales[:], in_=w2_grouped[:])
+
+        h_in, res_in, h_grouped, h_packed = {}, {}, {}, {}
+        res_biased, res2_of, neg_mean_of, std_of, normed_of = {}, {}, {}, {}, {}
+        n_grouped, n_packed, heads = {}, {}, {}
+
+        def load(g):
+            h_sb = loads.tile([P, GROUP * FFN], BF16)
+            nc.sync.dma_start(out=h_sb[:], in_=h_rows[:, g * GROUP * FFN : (g + 1) * GROUP * FFN])
+            res_sb = loads.tile([P, GROUP * MID], BF16)
+            nc.sync.dma_start(out=res_sb[:], in_=res_rows[:, g * GROUP * MID : (g + 1) * GROUP * MID])
+            h_in[g], res_in[g] = h_sb, res_sb
+
+        def transpose_h(g):
+            h_grouped[g] = transpose_bf16_rows(nc, psum, work, h_in[g][:], ident[:])
+
+        def quantise_h_and_bias_residual(g):
+            h_codes = work.tile([P, GROUP * P], U32, align_bytes=64)
+            h_scales = work.tile([P, GROUP * P], U8, align_bytes=64)
+            nc.vector.quantize_mx(out=h_codes[:].bitcast(FP8X4), scales=h_scales[:], in_=h_grouped[g][:])
+            h_packed[g] = (h_codes, h_scales)
+            res_b = work.tile([P, GROUP, MID], F32)
+            nc.vector.tensor_tensor(
+                out=res_b[:],
+                in0=res_in[g][:].rearrange("p (j m) -> p j m", j=GROUP),
+                in1=b1_all[:].unsqueeze(1).to_broadcast([P, GROUP, MID]),
+                op=ADD,
+            )
+            res_biased[g] = res_b
+
+        def first_matmul(g):
+            h_codes, h_scales = h_packed[g]
+            res2 = work.tile([P, GROUP, MID], F32)
+            sums = work.tile([P, GROUP], F32)
+            for j in range(GROUP):
+                tokens = slice(j * P, (j + 1) * P)
+                ffn = psum.tile([P, MID], F32)
+                nc.tensor.matmul_mx(
+                    out=ffn[:],
+                    lhsT=h_codes[:, tokens].bitcast(FP8X4),
+                    lhsT_scale=h_scales[:, tokens],
+                    rhs=w1_codes[:].bitcast(FP8X4),
+                    rhs_scale=w1_scales[:],
+                    start=True,
+                    stop=True,
+                )
+                nc.vector.scalar_tensor_tensor(
+                    out=res2[:, j, :], in0=ffn[:], scalar=1.0, in1=res_biased[g][:, j, :], op0=MULT, op1=ADD,
+                    accum_out=sums[:, j : j + 1],
+                )
+            neg_mean = work.tile([P, GROUP], F32)
+            nc.vector.tensor_scalar_mul(out=neg_mean[:], in0=sums[:], scalar1=-1.0 / MID)
+            res2_of[g], neg_mean_of[g] = res2, neg_mean
+
+        def deviation(g):
+            squares = work.tile([P, GROUP, MID], BF16)
+            square_sums = work.tile([P, GROUP], F32)
+            for j in range(GROUP):
+                nc.scalar.activation(
+                    out=squares[:, j, :], in_=res2_of[g][:, j, :], func=ACT.Square,
+                    bias=neg_mean_of[g][:, j : j + 1], scale=1.0, accum_out=square_sums[:, j : j + 1],
+                )
+            std = work.tile([P, GROUP], F32)
+            nc.scalar.activation(out=std[:], in_=square_sums[:], func=ACT.Sqrt, scale=1.0 / MID, bias=eps[:, 0:1])
+            std_of[g] = std
+
+        def normalise(g):
+            rstd = work.tile([P, GROUP], F32)
+            nc.vector.reciprocal(out=rstd[:], in_=std_of[g][:])
+            normed = work.tile([P, GROUP, MID], F32)
+            for j in range(GROUP):
+                nc.vector.tensor_scalar(
+                    out=normed[:, j, :], in0=res2_of[g][:, j, :], scalar1=neg_mean_of[g][:, j : j + 1],
+                    scalar2=rstd[:, j : j + 1], op0=ADD, op1=MULT,
+                )
+            normed_of[g] = normed
+
+        def transpose_norm(g):
+            n_grouped[g] = transpose_f32_rows(
+                nc, psum, work, [normed_of[g][:, j, :] for j in range(GROUP)], ident[:], gain, shift
+            )
+
+        def quantise_norm(g):
+            n_codes = work.tile([P, GROUP * P], U32, align_bytes=64)
+            n_scales = work.tile([P, GROUP * P], U8, align_bytes=64)
+            nc.vector.quantize_mx(out=n_codes[:].bitcast(FP8X4), scales=n_scales[:], in_=n_grouped[g][:])
+            n_packed[g] = (n_codes, n_scales)
+
+        def second_matmul(g):
+            n_codes, n_scales = n_packed[g]
+            heads[g] = []
+            for b in range(GROUP // 2):
+                head = psum.tile([P, 2, D_OUT], F32)
+                for j in range(2):
+                    tokens = slice((2 * b + j) * P, (2 * b + j + 1) * P)
+                    nc.tensor.matmul_mx(
+                        out=head[:, j, :],
+                        lhsT=n_codes[:, tokens].bitcast(FP8X4),
+                        lhsT_scale=n_scales[:, tokens],
+                        rhs=w2_codes[:].bitcast(FP8X4),
+                        rhs_scale=w2_scales[:],
+                        start=True,
+                        stop=True,
+                    )
+                heads[g].append(head)
+
+        def bias_and_store(g):
+            result = work.tile([P, GROUP, D_OUT], F32)
+            for b, head in enumerate(heads[g]):
+                nc.vector.tensor_tensor(
+                    out=result[:, 2 * b : 2 * b + 2, :],
+                    in0=head[:],
+                    in1=b2_all[:].unsqueeze(1).to_broadcast([P, 2, D_OUT]),
+                    op=ADD,
+                )
+            nc.gpsimd.dma_start(
+                out=out_rows[:, g * GROUP * D_OUT : (g + 1) * GROUP * D_OUT],
+                in_=result[:].rearrange("p j o -> p (j o)"),
+            )
+
+        def live(g):
+            return 0 <= g < GROUPS
+
+        for k in range(-2, GROUPS + 5):
+            if live(k + 2):
+                load(k + 2)
+            if live(k):
+                transpose_h(k)
+            if live(k - 4):
+                transpose_norm(k - 4)
+            if live(k - 1):
+                quantise_h_and_bias_residual(k - 1)
+            if live(k - 5):
+                quantise_norm(k - 5)
+            if live(k - 3):
+                normalise(k - 3)
+            if live(k - 1):
+                first_matmul(k - 1)
+            if live(k - 5):
+                second_matmul(k - 5)
+            if live(k - 2):
+                deviation(k - 2)
+            if live(k - 5):
+                bias_and_store(k - 5)

@@ -51,9 +51,13 @@ def transpose_f32_rows(nc, psum, work, row_tiles, ident, gain, shift):
             nc.tensor.transpose(chunk_t[:, r * P : (r + 1) * P], x[:, c * P : (c + 1) * P], ident)
         nc.scalar.activation(out=planes[:, c, :], in_=chunk_t[:], func=ACT.Identity, scale=gain[c], bias=shift[c])
     chunk_grouped = work.tile([P, width * PACK], BF16, align_bytes=64)
-    nc.scalar.copy(
+    nc.gpsimd.tensor_scalar(
         out=chunk_grouped[:].rearrange("p (w i c) -> p w c i", i=4, c=PACK),
-        in_=planes[:].rearrange("p c (w i) -> p w c i", i=4),
+        in0=planes[:].rearrange("p c (w i) -> p w c i", i=4),
+        scalar1=1.0,
+        scalar2=0.0,
+        op0=MULT,
+        op1=ADD,
     )
     return chunk_grouped
 
@@ -69,6 +73,7 @@ def tile_tsh_mid_block_pb_t_kernel(tc, h, w_f2, b_f2, res1, g2, be2, w_h, b_h, o
         loads = ctx.enter_context(tc.tile_pool(name="loads", bufs=4))
         work = ctx.enter_context(tc.tile_pool(name="work", bufs=3))
         psum = ctx.enter_context(tc.psum_pool(name="psum", bufs=2))
+        psum_single = ctx.enter_context(tc.psum_pool(name="psum_single", bufs=1))
 
         ident = const.tile([P, P], F32)
         make_identity(nc, ident[:])
@@ -90,10 +95,8 @@ def tile_tsh_mid_block_pb_t_kernel(tc, h, w_f2, b_f2, res1, g2, be2, w_h, b_h, o
         nc.scalar.dma_start(out=bias_rows[0:1, MID : MID + D_OUT], in_=b_h.rearrange("(o m) -> o m", o=1))
         ones = const.tile([P, P], BF16)
         nc.vector.memset(ones[:], 1.0)
-        b1_all = const.tile([P, MID], F32)
-        b1_spread = psum.tile([P, MID], F32, tag="ffn")
-        nc.tensor.matmul(out=b1_spread[:], lhsT=ones[:], rhs=bias_rows[:, 0:MID], start=True, stop=True)
-        nc.vector.tensor_copy(out=b1_all[:], in_=b1_spread[:])
+        b1_all = psum_single.tile([P, MID], F32)
+        nc.tensor.matmul(out=b1_all[:], lhsT=ones[:], rhs=bias_rows[:, 0:MID], start=True, stop=True)
         b2_all = const.tile([P, D_OUT], F32)
         b2_spread = psum.tile([P, D_OUT], F32, tag="ffn")
         nc.tensor.matmul(out=b2_spread[:], lhsT=ones[:], rhs=bias_rows[:, MID : MID + D_OUT], start=True, stop=True)
@@ -125,7 +128,7 @@ def tile_tsh_mid_block_pb_t_kernel(tc, h, w_f2, b_f2, res1, g2, be2, w_h, b_h, o
 
         h_in, res_in, h_grouped, h_packed = {}, {}, {}, {}
         res_biased, res2_of, neg_mean_of, std_of, normed_of = {}, {}, {}, {}, {}
-        n_grouped, n_packed, heads = {}, {}, {}
+        n_grouped, n_packed = {}, {}
 
         def load(g):
             h_sb = loads.tile([P, GROUP * FFN], BF16)
@@ -192,7 +195,7 @@ def tile_tsh_mid_block_pb_t_kernel(tc, h, w_f2, b_f2, res1, g2, be2, w_h, b_h, o
             nc.vector.reciprocal(out=rstd[:], in_=std_of[g][:])
             normed = work.tile([P, GROUP, MID], F32)
             for j in range(GROUP):
-                nc.vector.tensor_scalar(
+                nc.gpsimd.tensor_scalar(
                     out=normed[:, j, :], in0=res2_of[g][:, j, :], scalar1=neg_mean_of[g][:, j : j + 1],
                     scalar2=rstd[:, j : j + 1], op0=ADD, op1=MULT,
                 )
@@ -211,9 +214,9 @@ def tile_tsh_mid_block_pb_t_kernel(tc, h, w_f2, b_f2, res1, g2, be2, w_h, b_h, o
 
         def second_matmul(g):
             n_codes, n_scales = n_packed[g]
-            heads[g] = []
+            result = work.tile([P, GROUP, D_OUT], F32)
             for b in range(GROUP // 2):
-                head = psum.tile([P, 2, D_OUT], F32)
+                head = psum_single.tile([P, 2, D_OUT], F32)
                 for j in range(2):
                     tokens = slice((2 * b + j) * P, (2 * b + j + 1) * P)
                     nc.tensor.matmul_mx(
@@ -225,18 +228,13 @@ def tile_tsh_mid_block_pb_t_kernel(tc, h, w_f2, b_f2, res1, g2, be2, w_h, b_h, o
                         start=True,
                         stop=True,
                     )
-                heads[g].append(head)
-
-        def bias_and_store(g):
-            result = work.tile([P, GROUP, D_OUT], F32)
-            for b, head in enumerate(heads[g]):
                 nc.vector.tensor_tensor(
                     out=result[:, 2 * b : 2 * b + 2, :],
                     in0=head[:],
                     in1=b2_all[:].unsqueeze(1).to_broadcast([P, 2, D_OUT]),
                     op=ADD,
                 )
-            nc.gpsimd.dma_start(
+            nc.sync.dma_start(
                 out=out_rows[:, g * GROUP * D_OUT : (g + 1) * GROUP * D_OUT],
                 in_=result[:].rearrange("p j o -> p (j o)"),
             )
@@ -259,9 +257,7 @@ def tile_tsh_mid_block_pb_t_kernel(tc, h, w_f2, b_f2, res1, g2, be2, w_h, b_h, o
                 normalise(k - 3)
             if live(k - 1):
                 first_matmul(k - 1)
-            if live(k - 5):
-                second_matmul(k - 5)
             if live(k - 2):
                 deviation(k - 2)
             if live(k - 5):
-                bias_and_store(k - 5)
+                second_matmul(k - 5)

@@ -14,6 +14,7 @@ ACT = mybir.ActivationFunctionType
 
 P = 128
 PACK = 4
+BANK = 512
 TOKENS = 8 * 1024
 FFN = 512
 MID = 512
@@ -25,12 +26,12 @@ GROUPS = TOKENS // (P * GROUP)
 FLOPS = 2 * TOKENS * FFN * MID + 2 * TOKENS * MID * D_OUT
 
 
-def transpose_bf16_rows(nc, psum, work, rows, ident):
+def transpose_bf16_rows(nc, new_bank, work, rows, ident):
     words = rows.bitcast(F32)
     pair_grouped = work.tile([P, GROUP * P * PACK], BF16, align_bytes=64)
     grouped_words = pair_grouped[:].bitcast(F32).rearrange("p (j r u) -> p j r u", j=GROUP, u=2)
     for b in range(GROUP // 2):
-        pairs_t = psum.tile([P, 4 * P], F32)
+        pairs_t = new_bank()
         for j in range(2):
             for u in range(2):
                 first = ((2 * b + j) * 2 + u) * P
@@ -42,18 +43,24 @@ def transpose_bf16_rows(nc, psum, work, rows, ident):
     return pair_grouped
 
 
-def transpose_f32_rows(nc, psum, work, row_tiles, ident, gain, shift):
+def transpose_f32_rows(nc, new_bank, work, row_tiles, ident, gain, shift):
     width = len(row_tiles) * P
     planes = work.tile([P, PACK, width], BF16)
     for c in range(PACK):
-        chunk_t = psum.tile([P, width], F32)
+        chunk_t = new_bank()
         for r, x in enumerate(row_tiles):
             nc.tensor.transpose(chunk_t[:, r * P : (r + 1) * P], x[:, c * P : (c + 1) * P], ident)
-        nc.scalar.activation(out=planes[:, c, :], in_=chunk_t[:], func=ACT.Identity, scale=gain[c], bias=shift[c])
+        nc.scalar.activation(
+            out=planes[:, c, :], in_=chunk_t[:, 0:width], func=ACT.Identity, scale=gain[c], bias=shift[c]
+        )
+    return planes
+
+
+def group_planes(nc, work, planes, width):
     chunk_grouped = work.tile([P, width * PACK], BF16, align_bytes=64)
     nc.gpsimd.tensor_scalar(
-        out=chunk_grouped[:].rearrange("p (w i c) -> p w c i", i=4, c=PACK),
-        in0=planes[:].rearrange("p c (w i) -> p w c i", i=4),
+        out=chunk_grouped[:].rearrange("p (w c) -> p w c", c=PACK),
+        in0=planes[:].rearrange("p c w -> p w c"),
         scalar1=1.0,
         scalar2=0.0,
         op0=MULT,
@@ -72,8 +79,11 @@ def tile_tsh_mid_block_pb_t_kernel(tc, h, w_f2, b_f2, res1, g2, be2, w_h, b_h, o
         const = ctx.enter_context(tc.tile_pool(name="const", bufs=1))
         loads = ctx.enter_context(tc.tile_pool(name="loads", bufs=4))
         work = ctx.enter_context(tc.tile_pool(name="work", bufs=3))
-        psum = ctx.enter_context(tc.psum_pool(name="psum", bufs=2))
-        psum_single = ctx.enter_context(tc.psum_pool(name="psum_single", bufs=1))
+        bias_bank = ctx.enter_context(tc.psum_pool(name="bias_bank", bufs=1))
+        ring = ctx.enter_context(tc.psum_pool(name="ring", bufs=7))
+
+        def new_bank():
+            return ring.tile([P, BANK], F32, name="bank", tag="bank")
 
         ident = const.tile([P, P], F32)
         make_identity(nc, ident[:])
@@ -86,7 +96,7 @@ def tile_tsh_mid_block_pb_t_kernel(tc, h, w_f2, b_f2, res1, g2, be2, w_h, b_h, o
         )
         w1_codes = const.tile([P, MID], U32, align_bytes=64)
         w1_scales = const.tile([P, MID], U8, align_bytes=64)
-        w1_grouped = transpose_bf16_rows(nc, psum, work, w1_sb[:], ident[:])
+        w1_grouped = transpose_bf16_rows(nc, new_bank, work, w1_sb[:], ident[:])
         nc.vector.quantize_mx(out=w1_codes[:].bitcast(FP8X4), scales=w1_scales[:], in_=w1_grouped[:])
 
         bias_rows = const.tile([P, MID + D_OUT], BF16)
@@ -95,12 +105,14 @@ def tile_tsh_mid_block_pb_t_kernel(tc, h, w_f2, b_f2, res1, g2, be2, w_h, b_h, o
         nc.scalar.dma_start(out=bias_rows[0:1, MID : MID + D_OUT], in_=b_h.rearrange("(o m) -> o m", o=1))
         ones = const.tile([P, P], BF16)
         nc.vector.memset(ones[:], 1.0)
-        b1_all = psum_single.tile([P, MID], F32)
+        b1_all = bias_bank.tile([P, MID], F32)
         nc.tensor.matmul(out=b1_all[:], lhsT=ones[:], rhs=bias_rows[:, 0:MID], start=True, stop=True)
         b2_all = const.tile([P, D_OUT], F32)
-        b2_spread = psum.tile([P, D_OUT], F32, tag="ffn")
-        nc.tensor.matmul(out=b2_spread[:], lhsT=ones[:], rhs=bias_rows[:, MID : MID + D_OUT], start=True, stop=True)
-        nc.vector.tensor_copy(out=b2_all[:], in_=b2_spread[:])
+        b2_spread = new_bank()
+        nc.tensor.matmul(
+            out=b2_spread[:, 0:D_OUT], lhsT=ones[:], rhs=bias_rows[:, MID : MID + D_OUT], start=True, stop=True
+        )
+        nc.vector.tensor_copy(out=b2_all[:], in_=b2_spread[:, 0:D_OUT])
 
         vec_rows = const.tile([P, P], BF16)
         nc.vector.memset(vec_rows[:], 0.0)
@@ -108,8 +120,8 @@ def tile_tsh_mid_block_pb_t_kernel(tc, h, w_f2, b_f2, res1, g2, be2, w_h, b_h, o
         nc.scalar.dma_start(out=vec_rows[PACK : 2 * PACK, :], in_=be2.rearrange("(c p) -> c p", p=P))
         vec_rows_f32 = const.tile([P, P], F32)
         nc.vector.tensor_copy(out=vec_rows_f32[:], in_=vec_rows[:])
-        vec_t = psum.tile([P, P], F32, tag="chunk_t")
-        nc.tensor.transpose(vec_t[:], vec_rows_f32[:], ident[:])
+        vec_t = new_bank()
+        nc.tensor.transpose(vec_t[:, 0:P], vec_rows_f32[:], ident[:])
         vec_cols = const.tile([P, 2 * PACK], F32)
         nc.vector.tensor_copy(out=vec_cols[:], in_=vec_t[:, 0 : 2 * PACK])
         gain = [vec_cols[:, c : c + 1] for c in range(PACK)]
@@ -121,14 +133,15 @@ def tile_tsh_mid_block_pb_t_kernel(tc, h, w_f2, b_f2, res1, g2, be2, w_h, b_h, o
         nc.vector.tensor_copy(out=w2_f32[:], in_=w2_sb[:])
         w2_codes = const.tile([P, D_OUT], U32, align_bytes=64)
         w2_scales = const.tile([P, D_OUT], U8, align_bytes=64)
-        w2_grouped = transpose_f32_rows(
-            nc, psum, work, [w2_f32[:, r, :] for r in range(D_OUT // P)], ident[:], [1.0] * PACK, [0.0] * PACK
+        w2_planes = transpose_f32_rows(
+            nc, new_bank, work, [w2_f32[:, r, :] for r in range(D_OUT // P)], ident[:], [1.0] * PACK, [0.0] * PACK
         )
+        w2_grouped = group_planes(nc, work, w2_planes, D_OUT)
         nc.vector.quantize_mx(out=w2_codes[:].bitcast(FP8X4), scales=w2_scales[:], in_=w2_grouped[:])
 
         h_in, res_in, h_grouped, h_packed = {}, {}, {}, {}
         res_biased, res2_of, neg_mean_of, std_of, normed_of = {}, {}, {}, {}, {}
-        n_grouped, n_packed = {}, {}
+        n_planes, n_grouped, n_packed = {}, {}, {}
 
         def load(g):
             h_sb = loads.tile([P, GROUP * FFN], BF16)
@@ -138,13 +151,9 @@ def tile_tsh_mid_block_pb_t_kernel(tc, h, w_f2, b_f2, res1, g2, be2, w_h, b_h, o
             h_in[g], res_in[g] = h_sb, res_sb
 
         def transpose_h(g):
-            h_grouped[g] = transpose_bf16_rows(nc, psum, work, h_in[g][:], ident[:])
+            h_grouped[g] = transpose_bf16_rows(nc, new_bank, work, h_in[g][:], ident[:])
 
-        def quantise_h_and_bias_residual(g):
-            h_codes = work.tile([P, GROUP * P], U32, align_bytes=64)
-            h_scales = work.tile([P, GROUP * P], U8, align_bytes=64)
-            nc.vector.quantize_mx(out=h_codes[:].bitcast(FP8X4), scales=h_scales[:], in_=h_grouped[g][:])
-            h_packed[g] = (h_codes, h_scales)
+        def bias_residual(g):
             res_b = work.tile([P, GROUP, MID], F32)
             nc.vector.tensor_tensor(
                 out=res_b[:],
@@ -154,13 +163,19 @@ def tile_tsh_mid_block_pb_t_kernel(tc, h, w_f2, b_f2, res1, g2, be2, w_h, b_h, o
             )
             res_biased[g] = res_b
 
+        def quantise_h(g):
+            h_codes = work.tile([P, GROUP * P], U32, align_bytes=64)
+            h_scales = work.tile([P, GROUP * P], U8, align_bytes=64)
+            nc.vector.quantize_mx(out=h_codes[:].bitcast(FP8X4), scales=h_scales[:], in_=h_grouped[g][:])
+            h_packed[g] = (h_codes, h_scales)
+
         def first_matmul(g):
             h_codes, h_scales = h_packed[g]
             res2 = work.tile([P, GROUP, MID], F32)
             sums = work.tile([P, GROUP], F32)
             for j in range(GROUP):
                 tokens = slice(j * P, (j + 1) * P)
-                ffn = psum.tile([P, MID], F32)
+                ffn = new_bank()
                 nc.tensor.matmul_mx(
                     out=ffn[:],
                     lhsT=h_codes[:, tokens].bitcast(FP8X4),
@@ -193,18 +208,27 @@ def tile_tsh_mid_block_pb_t_kernel(tc, h, w_f2, b_f2, res1, g2, be2, w_h, b_h, o
         def normalise(g):
             rstd = work.tile([P, GROUP], F32)
             nc.vector.reciprocal(out=rstd[:], in_=std_of[g][:])
+            offset = work.tile([P, GROUP], F32)
+            nc.vector.tensor_tensor(out=offset[:], in0=neg_mean_of[g][:], in1=rstd[:], op=MULT)
             normed = work.tile([P, GROUP, MID], F32)
-            for j in range(GROUP):
+            for j in range(0, GROUP, 2):
                 nc.gpsimd.tensor_scalar(
-                    out=normed[:, j, :], in0=res2_of[g][:, j, :], scalar1=neg_mean_of[g][:, j : j + 1],
-                    scalar2=rstd[:, j : j + 1], op0=ADD, op1=MULT,
+                    out=normed[:, j, :], in0=res2_of[g][:, j, :], scalar1=rstd[:, j : j + 1],
+                    scalar2=offset[:, j : j + 1], op0=MULT, op1=ADD,
+                )
+                nc.scalar.activation(
+                    out=normed[:, j + 1, :], in_=res2_of[g][:, j + 1, :], func=ACT.Identity,
+                    scale=rstd[:, j + 1 : j + 2], bias=offset[:, j + 1 : j + 2],
                 )
             normed_of[g] = normed
 
         def transpose_norm(g):
-            n_grouped[g] = transpose_f32_rows(
-                nc, psum, work, [normed_of[g][:, j, :] for j in range(GROUP)], ident[:], gain, shift
+            n_planes[g] = transpose_f32_rows(
+                nc, new_bank, work, [normed_of[g][:, j, :] for j in range(GROUP)], ident[:], gain, shift
             )
+
+        def group_norm(g):
+            n_grouped[g] = group_planes(nc, work, n_planes[g], GROUP * P)
 
         def quantise_norm(g):
             n_codes = work.tile([P, GROUP * P], U32, align_bytes=64)
@@ -216,11 +240,11 @@ def tile_tsh_mid_block_pb_t_kernel(tc, h, w_f2, b_f2, res1, g2, be2, w_h, b_h, o
             n_codes, n_scales = n_packed[g]
             result = work.tile([P, GROUP, D_OUT], F32)
             for b in range(GROUP // 2):
-                head = psum_single.tile([P, 2, D_OUT], F32)
+                head = new_bank()
                 for j in range(2):
                     tokens = slice((2 * b + j) * P, (2 * b + j + 1) * P)
                     nc.tensor.matmul_mx(
-                        out=head[:, j, :],
+                        out=head[:, j * D_OUT : (j + 1) * D_OUT],
                         lhsT=n_codes[:, tokens].bitcast(FP8X4),
                         lhsT_scale=n_scales[:, tokens],
                         rhs=w2_codes[:].bitcast(FP8X4),
@@ -230,7 +254,7 @@ def tile_tsh_mid_block_pb_t_kernel(tc, h, w_f2, b_f2, res1, g2, be2, w_h, b_h, o
                     )
                 nc.vector.tensor_tensor(
                     out=result[:, 2 * b : 2 * b + 2, :],
-                    in0=head[:],
+                    in0=head[:].rearrange("p (j o) -> p j o", j=2),
                     in1=b2_all[:].unsqueeze(1).to_broadcast([P, 2, D_OUT]),
                     op=ADD,
                 )
@@ -242,22 +266,27 @@ def tile_tsh_mid_block_pb_t_kernel(tc, h, w_f2, b_f2, res1, g2, be2, w_h, b_h, o
         def live(g):
             return 0 <= g < GROUPS
 
-        for k in range(-2, GROUPS + 5):
-            if live(k + 2):
-                load(k + 2)
-            if live(k):
-                transpose_h(k)
-            if live(k - 4):
-                transpose_norm(k - 4)
-            if live(k - 1):
-                quantise_h_and_bias_residual(k - 1)
-            if live(k - 5):
-                quantise_norm(k - 5)
-            if live(k - 3):
-                normalise(k - 3)
-            if live(k - 1):
-                first_matmul(k - 1)
-            if live(k - 2):
-                deviation(k - 2)
-            if live(k - 5):
-                second_matmul(k - 5)
+        with tc.manual_schedule():
+            for k in range(GROUPS + 6):
+                if live(k - 2):
+                    transpose_h(k - 2)
+                if live(k - 4):
+                    deviation(k - 4)
+                if live(k - 5):
+                    transpose_norm(k - 5)
+                if live(k - 3):
+                    bias_residual(k - 3)
+                if live(k - 2):
+                    quantise_h(k - 2)
+                if live(k - 6):
+                    quantise_norm(k - 6)
+                if live(k):
+                    load(k)
+                if live(k - 4):
+                    normalise(k - 4)
+                if live(k - 3):
+                    first_matmul(k - 3)
+                if live(k - 5):
+                    group_norm(k - 5)
+                if live(k - 6):
+                    second_matmul(k - 6)

@@ -140,7 +140,7 @@ def tile_tsh_mid_block_pb_t_kernel(tc, h, w_f2, b_f2, res1, g2, be2, w_h, b_h, o
         nc.vector.quantize_mx(out=w2_codes[:].bitcast(FP8X4), scales=w2_scales[:], in_=w2_grouped[:])
 
         h_in, res_in, h_grouped, h_packed = {}, {}, {}, {}
-        res_biased, res2_of, neg_mean_of, std_of, normed_of = {}, {}, {}, {}, {}
+        res_biased, res2_of, sums_of, neg_mean_of, std_of, normed_of = {}, {}, {}, {}, {}, {}
         n_planes, n_grouped, n_packed = {}, {}, {}
 
         def load(g):
@@ -189,9 +189,12 @@ def tile_tsh_mid_block_pb_t_kernel(tc, h, w_f2, b_f2, res1, g2, be2, w_h, b_h, o
                     out=res2[:, j, :], in0=ffn[:], scalar=1.0, in1=res_biased[g][:, j, :], op0=MULT, op1=ADD,
                     accum_out=sums[:, j : j + 1],
                 )
+            res2_of[g], sums_of[g] = res2, sums
+
+        def negative_mean(g):
             neg_mean = work.tile([P, GROUP], F32)
-            nc.vector.tensor_scalar_mul(out=neg_mean[:], in0=sums[:], scalar1=-1.0 / MID)
-            res2_of[g], neg_mean_of[g] = res2, neg_mean
+            nc.scalar.mul(out=neg_mean[:], in_=sums_of[g][:], mul=-1.0 / MID)
+            neg_mean_of[g] = neg_mean
 
         def deviation(g):
             squares = work.tile([P, GROUP, MID], BF16)
@@ -268,6 +271,8 @@ def tile_tsh_mid_block_pb_t_kernel(tc, h, w_f2, b_f2, res1, g2, be2, w_h, b_h, o
 
         with tc.manual_schedule():
             for k in range(GROUPS + 6):
+                if live(k - 4):
+                    negative_mean(k - 4)
                 if live(k - 2):
                     transpose_h(k - 2)
                 if live(k - 4):

@@ -22,6 +22,7 @@ D_OUT = 256
 LN_EPS = 1e-5
 GROUP = 4
 GROUPS = TOKENS // (P * GROUP)
+GPSIMD_TILES = 3
 
 FLOPS = 2 * TOKENS * FFN * MID + 2 * TOKENS * MID * D_OUT
 
@@ -214,14 +215,15 @@ def tile_tsh_mid_block_pb_t_kernel(tc, h, w_f2, b_f2, res1, g2, be2, w_h, b_h, o
             offset = work.tile([P, GROUP], F32)
             nc.vector.tensor_tensor(out=offset[:], in0=neg_mean_of[g][:], in1=rstd[:], op=MULT)
             normed = work.tile([P, GROUP, MID], F32)
-            for j in range(0, GROUP, 2):
+            for j in range(GPSIMD_TILES):
                 nc.gpsimd.tensor_scalar(
                     out=normed[:, j, :], in0=res2_of[g][:, j, :], scalar1=rstd[:, j : j + 1],
                     scalar2=offset[:, j : j + 1], op0=MULT, op1=ADD,
                 )
+            for j in range(GPSIMD_TILES, GROUP):
                 nc.scalar.activation(
-                    out=normed[:, j + 1, :], in_=res2_of[g][:, j + 1, :], func=ACT.Identity,
-                    scale=rstd[:, j + 1 : j + 2], bias=offset[:, j + 1 : j + 2],
+                    out=normed[:, j, :], in_=res2_of[g][:, j, :], func=ACT.Identity,
+                    scale=rstd[:, j : j + 1], bias=offset[:, j : j + 1],
                 )
             normed_of[g] = normed
 

@@ -272,28 +272,27 @@ def tile_tsh_mid_block_pb_t_kernel(tc, h, w_f2, b_f2, res1, g2, be2, w_h, b_h, o
             return 0 <= g < GROUPS
 
         with tc.manual_schedule():
-            for k in range(GROUPS + 6):
-                if live(k - 4):
-                    negative_mean(k - 4)
+            for k in range(GROUPS + 7):
+                if live(k - 5):
+                    negative_mean(k - 5)
+                    deviation(k - 5)
                 if live(k - 2):
                     transpose_h(k - 2)
-                if live(k - 4):
-                    deviation(k - 4)
-                if live(k - 5):
-                    transpose_norm(k - 5)
-                if live(k - 3):
-                    bias_residual(k - 3)
-                if live(k - 2):
-                    quantise_h(k - 2)
                 if live(k - 6):
-                    quantise_norm(k - 6)
+                    transpose_norm(k - 6)
+                if live(k - 4):
+                    bias_residual(k - 4)
+                if live(k - 3):
+                    quantise_h(k - 3)
+                if live(k - 7):
+                    quantise_norm(k - 7)
                 if live(k):
                     load(k)
-                if live(k - 4):
-                    normalise(k - 4)
-                if live(k - 3):
-                    first_matmul(k - 3)
                 if live(k - 5):
-                    group_norm(k - 5)
+                    normalise(k - 5)
+                if live(k - 4):
+                    first_matmul(k - 4)
                 if live(k - 6):
-                    second_matmul(k - 6)
+                    group_norm(k - 6)
+                if live(k - 7):
+                    second_matmul(k - 7)

from contextlib import ExitStack

import concourse.mybir as mybir
from concourse.masks import make_identity

F32 = mybir.dt.float32
BF16 = mybir.dt.bfloat16
U32 = mybir.dt.uint32
U8 = mybir.dt.uint8
FP8X4 = mybir.dt.float8_e4m3fn_x4
ADD = mybir.AluOpType.add
MULT = mybir.AluOpType.mult
ACT = mybir.ActivationFunctionType

P = 128
PACK = 4
BANK = 512
TOKENS = 8 * 1024
FFN = 512
MID = 512
D_OUT = 256
LN_EPS = 1e-5
GROUP = 4
GROUPS = TOKENS // (P * GROUP)
GPSIMD_TILES = 3

FLOPS = 2 * TOKENS * FFN * MID + 2 * TOKENS * MID * D_OUT


def transpose_bf16_rows(nc, new_bank, work, rows, ident):
    words = rows.bitcast(F32)
    pair_grouped = work.tile([P, GROUP * P * PACK], BF16, align_bytes=64)
    grouped_words = pair_grouped[:].bitcast(F32).rearrange("p (j r u) -> p j r u", j=GROUP, u=2)
    for b in range(GROUP // 2):
        pairs_t = new_bank()
        for j in range(2):
            for u in range(2):
                first = ((2 * b + j) * 2 + u) * P
                nc.tensor.transpose(pairs_t[:, (2 * j + u) * P : (2 * j + u + 1) * P], words[:, first : first + P], ident)
        nc.scalar.copy(
            out=grouped_words[:, 2 * b : 2 * b + 2],
            in_=pairs_t[:].rearrange("p (j u r) -> p j r u", j=2, u=2),
        )
    return pair_grouped


def transpose_f32_rows(nc, new_bank, work, row_tiles, ident, gain, shift):
    width = len(row_tiles) * P
    planes = work.tile([P, PACK, width], BF16)
    for c in range(PACK):
        chunk_t = new_bank()
        for r, x in enumerate(row_tiles):
            nc.tensor.transpose(chunk_t[:, r * P : (r + 1) * P], x[:, c * P : (c + 1) * P], ident)
        nc.scalar.activation(
            out=planes[:, c, :], in_=chunk_t[:, 0:width], func=ACT.Identity, scale=gain[c], bias=shift[c]
        )
    return planes


def group_planes(nc, work, planes, width):
    chunk_grouped = work.tile([P, width * PACK], BF16, align_bytes=64)
    nc.gpsimd.tensor_scalar(
        out=chunk_grouped[:].rearrange("p (w c) -> p w c", c=PACK),
        in0=planes[:].rearrange("p c w -> p w c"),
        scalar1=1.0,
        scalar2=0.0,
        op0=MULT,
        op1=ADD,
    )
    return chunk_grouped


def tile_tsh_mid_block_pb_t_kernel(tc, h, w_f2, b_f2, res1, g2, be2, w_h, b_h, out):
    nc = tc.nc
    h_rows = h.flatten_outer_dims().rearrange("(p j) k -> p (j k)", p=P)
    res_rows = res1.flatten_outer_dims().rearrange("(p j) m -> p (j m)", p=P)
    out_rows = out.flatten_outer_dims().rearrange("(p j) o -> p (j o)", p=P)

    with ExitStack() as ctx:
        const = ctx.enter_context(tc.tile_pool(name="const", bufs=1))
        loads = ctx.enter_context(tc.tile_pool(name="loads", bufs=4))
        work = ctx.enter_context(tc.tile_pool(name="work", bufs=3))
        bias_bank = ctx.enter_context(tc.psum_pool(name="bias_bank", bufs=1))
        ring = ctx.enter_context(tc.psum_pool(name="ring", bufs=7))

        def new_bank():
            return ring.tile([P, BANK], F32, name="bank", tag="bank")

        ident = const.tile([P, P], F32)
        make_identity(nc, ident[:])
        eps = const.tile([P, 1], F32)
        nc.vector.memset(eps[:], LN_EPS)

        w1_sb = const.tile([P, GROUP * FFN], BF16)
        nc.sync.dma_start(
            out=w1_sb[:].rearrange("p (r k) -> p r k", r=GROUP), in_=w_f2.rearrange("(r p) k -> p r k", p=P)
        )
        w1_codes = const.tile([P, MID], U32, align_bytes=64)
        w1_scales = const.tile([P, MID], U8, align_bytes=64)
        w1_grouped = transpose_bf16_rows(nc, new_bank, work, w1_sb[:], ident[:])
        nc.vector.quantize_mx(out=w1_codes[:].bitcast(FP8X4), scales=w1_scales[:], in_=w1_grouped[:])

        bias_rows = const.tile([P, MID + D_OUT], BF16)
        nc.vector.memset(bias_rows[:], 0.0)
        nc.scalar.dma_start(out=bias_rows[0:1, 0:MID], in_=b_f2.rearrange("(o m) -> o m", o=1))
        nc.scalar.dma_start(out=bias_rows[0:1, MID : MID + D_OUT], in_=b_h.rearrange("(o m) -> o m", o=1))
        ones = const.tile([P, P], BF16)
        nc.vector.memset(ones[:], 1.0)
        b1_all = bias_bank.tile([P, MID], F32)
        nc.tensor.matmul(out=b1_all[:], lhsT=ones[:], rhs=bias_rows[:, 0:MID], start=True, stop=True)
        b2_all = const.tile([P, D_OUT], F32)
        b2_spread = new_bank()
        nc.tensor.matmul(
            out=b2_spread[:, 0:D_OUT], lhsT=ones[:], rhs=bias_rows[:, MID : MID + D_OUT], start=True, stop=True
        )
        nc.vector.tensor_copy(out=b2_all[:], in_=b2_spread[:, 0:D_OUT])

        vec_rows = const.tile([P, P], BF16)
        nc.vector.memset(vec_rows[:], 0.0)
        nc.scalar.dma_start(out=vec_rows[0:PACK, :], in_=g2.rearrange("(c p) -> c p", p=P))
        nc.scalar.dma_start(out=vec_rows[PACK : 2 * PACK, :], in_=be2.rearrange("(c p) -> c p", p=P))
        vec_rows_f32 = const.tile([P, P], F32)
        nc.vector.tensor_copy(out=vec_rows_f32[:], in_=vec_rows[:])
        vec_t = new_bank()
        nc.tensor.transpose(vec_t[:, 0:P], vec_rows_f32[:], ident[:])
        vec_cols = const.tile([P, 2 * PACK], F32)
        nc.vector.tensor_copy(out=vec_cols[:], in_=vec_t[:, 0 : 2 * PACK])
        gain = [vec_cols[:, c : c + 1] for c in range(PACK)]
        shift = [vec_cols[:, PACK + c : PACK + c + 1] for c in range(PACK)]

        w2_sb = const.tile([P, D_OUT // P, MID], BF16)
        nc.scalar.dma_start(out=w2_sb[:], in_=w_h.rearrange("(r p) m -> p r m", p=P))
        w2_f32 = const.tile([P, D_OUT // P, MID], F32)
        nc.vector.tensor_copy(out=w2_f32[:], in_=w2_sb[:])
        w2_codes = const.tile([P, D_OUT], U32, align_bytes=64)
        w2_scales = const.tile([P, D_OUT], U8, align_bytes=64)
        w2_planes = transpose_f32_rows(
            nc, new_bank, work, [w2_f32[:, r, :] for r in range(D_OUT // P)], ident[:], [1.0] * PACK, [0.0] * PACK
        )
        w2_grouped = group_planes(nc, work, w2_planes, D_OUT)
        nc.vector.quantize_mx(out=w2_codes[:].bitcast(FP8X4), scales=w2_scales[:], in_=w2_grouped[:])

        h_in, res_in, h_grouped, h_packed = {}, {}, {}, {}
        res_biased, res2_of, sums_of, neg_mean_of, std_of, normed_of = {}, {}, {}, {}, {}, {}
        n_planes, n_grouped, n_packed = {}, {}, {}

        def load(g):
            h_sb = loads.tile([P, GROUP * FFN], BF16)
            nc.sync.dma_start(out=h_sb[:], in_=h_rows[:, g * GROUP * FFN : (g + 1) * GROUP * FFN])
            res_sb = loads.tile([P, GROUP * MID], BF16)
            nc.sync.dma_start(out=res_sb[:], in_=res_rows[:, g * GROUP * MID : (g + 1) * GROUP * MID])
            h_in[g], res_in[g] = h_sb, res_sb

        def transpose_h(g):
            h_grouped[g] = transpose_bf16_rows(nc, new_bank, work, h_in[g][:], ident[:])

        def bias_residual(g):
            res_b = work.tile([P, GROUP, MID], F32)
            nc.vector.tensor_tensor(
                out=res_b[:],
                in0=res_in[g][:].rearrange("p (j m) -> p j m", j=GROUP),
                in1=b1_all[:].unsqueeze(1).to_broadcast([P, GROUP, MID]),
                op=ADD,
            )
            res_biased[g] = res_b

        def quantise_h(g):
            h_codes = work.tile([P, GROUP * P], U32, align_bytes=64)
            h_scales = work.tile([P, GROUP * P], U8, align_bytes=64)
            nc.vector.quantize_mx(out=h_codes[:].bitcast(FP8X4), scales=h_scales[:], in_=h_grouped[g][:])
            h_packed[g] = (h_codes, h_scales)

        def first_matmul(g):
            h_codes, h_scales = h_packed[g]
            res2 = work.tile([P, GROUP, MID], F32)
            sums = work.tile([P, GROUP], F32)
            for j in range(GROUP):
                tokens = slice(j * P, (j + 1) * P)
                ffn = new_bank()
                nc.tensor.matmul_mx(
                    out=ffn[:],
                    lhsT=h_codes[:, tokens].bitcast(FP8X4),
                    lhsT_scale=h_scales[:, tokens],
                    rhs=w1_codes[:].bitcast(FP8X4),
                    rhs_scale=w1_scales[:],
                    start=True,
                    stop=True,
                )
                nc.vector.scalar_tensor_tensor(
                    out=res2[:, j, :], in0=ffn[:], scalar=1.0, in1=res_biased[g][:, j, :], op0=MULT, op1=ADD,
                    accum_out=sums[:, j : j + 1],
                )
            res2_of[g], sums_of[g] = res2, sums

        def negative_mean(g):
            neg_mean = work.tile([P, GROUP], F32)
            nc.scalar.mul(out=neg_mean[:], in_=sums_of[g][:], mul=-1.0 / MID)
            neg_mean_of[g] = neg_mean

        def deviation(g):
            squares = work.tile([P, GROUP, MID], BF16)
            square_sums = work.tile([P, GROUP], F32)
            for j in range(GROUP):
                nc.scalar.activation(
                    out=squares[:, j, :], in_=res2_of[g][:, j, :], func=ACT.Square,
                    bias=neg_mean_of[g][:, j : j + 1], scale=1.0, accum_out=square_sums[:, j : j + 1],
                )
            std = work.tile([P, GROUP], F32)
            nc.scalar.activation(out=std[:], in_=square_sums[:], func=ACT.Sqrt, scale=1.0 / MID, bias=eps[:, 0:1])
            std_of[g] = std

        def normalise(g):
            rstd = work.tile([P, GROUP], F32)
            nc.vector.reciprocal(out=rstd[:], in_=std_of[g][:])
            offset = work.tile([P, GROUP], F32)
            nc.vector.tensor_tensor(out=offset[:], in0=neg_mean_of[g][:], in1=rstd[:], op=MULT)
            normed = work.tile([P, GROUP, MID], F32)
            for j in range(GPSIMD_TILES):
                nc.gpsimd.tensor_scalar(
                    out=normed[:, j, :], in0=res2_of[g][:, j, :], scalar1=rstd[:, j : j + 1],
                    scalar2=offset[:, j : j + 1], op0=MULT, op1=ADD,
                )
            for j in range(GPSIMD_TILES, GROUP):
                nc.scalar.activation(
                    out=normed[:, j, :], in_=res2_of[g][:, j, :], func=ACT.Identity,
                    scale=rstd[:, j : j + 1], bias=offset[:, j : j + 1],
                )
            normed_of[g] = normed

        def transpose_norm(g):
            n_planes[g] = transpose_f32_rows(
                nc, new_bank, work, [normed_of[g][:, j, :] for j in range(GROUP)], ident[:], gain, shift
            )

        def group_norm(g):
            n_grouped[g] = group_planes(nc, work, n_planes[g], GROUP * P)

        def quantise_norm(g):
            n_codes = work.tile([P, GROUP * P], U32, align_bytes=64)
            n_scales = work.tile([P, GROUP * P], U8, align_bytes=64)
            nc.vector.quantize_mx(out=n_codes[:].bitcast(FP8X4), scales=n_scales[:], in_=n_grouped[g][:])
            n_packed[g] = (n_codes, n_scales)

        def second_matmul(g):
            n_codes, n_scales = n_packed[g]
            result = work.tile([P, GROUP, D_OUT], F32)
            for b in range(GROUP // 2):
                head = new_bank()
                for j in range(2):
                    tokens = slice((2 * b + j) * P, (2 * b + j + 1) * P)
                    nc.tensor.matmul_mx(
                        out=head[:, j * D_OUT : (j + 1) * D_OUT],
                        lhsT=n_codes[:, tokens].bitcast(FP8X4),
                        lhsT_scale=n_scales[:, tokens],
                        rhs=w2_codes[:].bitcast(FP8X4),
                        rhs_scale=w2_scales[:],
                        start=True,
                        stop=True,
                    )
                nc.vector.tensor_tensor(
                    out=result[:, 2 * b : 2 * b + 2, :],
                    in0=head[:].rearrange("p (j o) -> p j o", j=2),
                    in1=b2_all[:].unsqueeze(1).to_broadcast([P, 2, D_OUT]),
                    op=ADD,
                )
            nc.sync.dma_start(
                out=out_rows[:, g * GROUP * D_OUT : (g + 1) * GROUP * D_OUT],
                in_=result[:].rearrange("p j o -> p (j o)"),
            )

        def live(g):
            return 0 <= g < GROUPS

        with tc.manual_schedule():
            for k in range(GROUPS + 7):
                if live(k - 5):
                    negative_mean(k - 5)
                    deviation(k - 5)
                if live(k - 2):
                    transpose_h(k - 2)
                if live(k - 6):
                    transpose_norm(k - 6)
                if live(k - 4):
                    bias_residual(k - 4)
                if live(k - 3):
                    quantise_h(k - 3)
                if live(k - 7):
                    quantise_norm(k - 7)
                if live(k):
                    load(k)
                if live(k - 5):
                    normalise(k - 5)
                if live(k - 4):
                    first_matmul(k - 4)
                if live(k - 6):
                    group_norm(k - 6)
                if live(k - 7):
                    second_matmul(k - 7)
